import numpy as np
import ml_dtypes

BF16 = ml_dtypes.bfloat16


def bf(x):
    return np.asarray(x, np.float32).astype(BF16)


def f32(x):
    return np.asarray(x, np.float32)


def f64(x):
    return np.asarray(x).astype(np.float64)


def striped(idx):
    return np.tile(idx.reshape(-1, 16).T, (8, 1))


D, S, M, N = 128, 512, 256, 128
SCALE = 1.0 / np.sqrt(D)


def setup_inputs():
    col = np.concatenate([np.full(D, 0.7), np.full(M - D, 1.0)])
    return {"table": bf(np.random.standard_normal((D, S))), "w": bf(np.random.standard_normal((D, M)) * col / np.sqrt(D)), "b": f32(0.1 * np.random.standard_normal((M, 1))), "attn_bias": f32(np.random.standard_normal((N, N))), "offs": striped(np.random.permutation(S)[:N])}


def reference(table, w, b, attn_bias, offs):
    idx = offs[:16].T.reshape(-1)
    y = f64(w).T @ f64(table)[:, idx] + f64(b)
    qk, v = y[:D], y[D:]
    sc = SCALE * (qk.T @ qk) + f64(attn_bias)
    e = np.exp(sc - sc.max(axis=1, keepdims=True))
    p = e / e.sum(axis=1, keepdims=True)
    return v @ p.T

@@ -1,0 +1,80 @@
+import math
+
+import concourse.mybir as mybir
+from concourse.masks import make_identity
+
+P = 128
+SLOTS = 512
+N = 128
+SCALE = 1.0 / math.sqrt(P)
+FLOPS = 2 * P * (2 * P) * N + 2 * P * N * N + 2 * N * N * P
+
+BF16 = mybir.dt.bfloat16
+F32 = mybir.dt.float32
+U16 = mybir.dt.uint16
+ALU = mybir.AluOpType
+ACT = mybir.ActivationFunctionType
+X = mybir.AxisListType.X
+
+
+def tile_bertunpadselfattention_kernel(tc, table, w, b, attn_bias, offs, out):
+    nc = tc.nc
+    with (
+        tc.tile_pool(name="held", bufs=1) as held,
+        tc.psum_pool(name="psum", bufs=1) as psum,
+    ):
+        offsets = held.tile([P, N // 16], U16, name="offsets")
+        nc.sync.dma_start(offsets[:], offs)
+        table_sb = held.tile([P, SLOTS], BF16, name="table_sb")
+        nc.sync.dma_start(table_sb[:], table)
+        w_sb = held.tile([P, 2 * P], BF16, name="w_sb")
+        nc.scalar.dma_start(w_sb[:], w)
+        b_sb = held.tile([P, 2], F32, name="b_sb")
+        with nc.allow_non_contiguous_dma(reason="256 floats, one to a partition and column"):
+            nc.scalar.dma_start(b_sb[:], b.rearrange("(h p) o -> p (h o)", p=P))
+        bias_sb = held.tile([P, N], F32, name="bias_sb")
+        nc.scalar.dma_start(bias_sb[:], attn_bias)
+
+        identity = held.tile([P, P], BF16, name="identity")
+        make_identity(nc, identity[:])
+
+        picked = table_sb[:].indirect(offsets[:])
+        qk_ps = psum.tile([P, N], F32, name="qk_ps")
+        nc.tensor.matmul(qk_ps[:], w_sb[:, 0:P], picked, start=True, stop=True)
+        v_ps = psum.tile([P, N], F32, name="v_ps")
+        nc.tensor.matmul(v_ps[:], w_sb[:, P : 2 * P], picked, start=True, stop=True)
+
+        qk = held.tile([P, N], BF16, name="qk")
+        nc.vector.tensor_scalar_add(qk[:], qk_ps[:], b_sb[:, 0:1])
+        v = held.tile([P, N], BF16, name="v")
+        nc.vector.tensor_scalar_add(v[:], v_ps[:], b_sb[:, 1:2])
+
+        dots_ps = psum.tile([N, N], F32, name="dots_ps")
+        nc.tensor.matmul(dots_ps[:], qk[:], qk[:], start=True, stop=True)
+
+        vT_ps = psum.tile([N, P], BF16, name="vT_ps")
+        nc.tensor.transpose(vT_ps[:], v[:], identity[:])
+        vT = held.tile([N, P], BF16, name="vT")
+        nc.vector.tensor_copy(vT[:], vT_ps[:])
+
+        sc = held.tile([N, N], F32, name="sc")
+        nc.vector.scalar_tensor_tensor(sc[:], dots_ps[:], SCALE, bias_sb[:], ALU.mult, ALU.add)
+        neg_max = held.tile([N, 1], F32, name="neg_max")
+        nc.vector.reduce_max(neg_max[:], sc[:], axis=X, negate=True)
+        e = held.tile([N, N], F32, name="e")
+        e_sum = held.tile([N, 1], F32, name="e_sum")
+        nc.scalar.activation(e[:], sc[:], ACT.Exp, bias=neg_max[:], scale=1.0, accum_out=e_sum[:])
+        inv_sum = held.tile([N, 1], F32, name="inv_sum")
+        nc.vector.reciprocal(inv_sum[:], e_sum[:])
+        p = held.tile([N, N], BF16, name="p")
+        nc.vector.tensor_scalar_mul(p[:], e[:], inv_sum[:])
+
+        pT_ps = psum.tile([N, N], BF16, name="pT_ps")
+        nc.tensor.transpose(pT_ps[:], p[:], identity[:])
+        pT = held.tile([N, N], BF16, name="pT")
+        nc.vector.tensor_copy(pT[:], pT_ps[:])
+        out_ps = psum.tile([P, N], F32, name="out_ps")
+        nc.tensor.matmul(out_ps[:], vT[:], pT[:], start=True, stop=True)
+        out_sb = held.tile([P, N], F32, name="out_sb")
+        nc.vector.tensor_copy(out_sb[:], out_ps[:])
+        nc.sync.dma_start(out, out_sb[:])

@@ -35,6 +35,10 @@ def tile_bertunpadselfattention_kernel(tc, table, w, b, attn_bias, offs, out):
         bias_sb = held.tile([P, N], F32, name="bias_sb")
         nc.scalar.dma_start(bias_sb[:], attn_bias)
 
+        warm = held.tile([P, 1], F32, name="warm")
+        nc.vector.memset(warm[:], 0.0)
+        nc.scalar.activation(warm[:], warm[:], ACT.Exp)
+
         identity = held.tile([P, P], BF16, name="identity")
         make_identity(nc, identity[:])
 
@@ -47,7 +51,7 @@ def tile_bertunpadselfattention_kernel(tc, table, w, b, attn_bias, offs, out):
         qk = held.tile([P, N], BF16, name="qk")
         nc.vector.tensor_scalar_add(qk[:], qk_ps[:], b_sb[:, 0:1])
         v = held.tile([P, N], BF16, name="v")
-        nc.vector.tensor_scalar_add(v[:], v_ps[:], b_sb[:, 1:2])
+        nc.scalar.activation(v[:], v_ps[:], ACT.Identity, bias=b_sb[:, 1:2])
 
         dots_ps = psum.tile([N, N], F32, name="dots_ps")
         nc.tensor.matmul(dots_ps[:], qk[:], qk[:], start=True, stop=True)
@@ -55,7 +59,7 @@ def tile_bertunpadselfattention_kernel(tc, table, w, b, attn_bias, offs, out):
         vT_ps = psum.tile([N, P], BF16, name="vT_ps")
         nc.tensor.transpose(vT_ps[:], v[:], identity[:])
         vT = held.tile([N, P], BF16, name="vT")
-        nc.vector.tensor_copy(vT[:], vT_ps[:])
+        nc.scalar.copy(vT[:], vT_ps[:])
 
         sc = held.tile([N, N], F32, name="sc")
         nc.vector.scalar_tensor_tensor(sc[:], dots_ps[:], SCALE, bias_sb[:], ALU.mult, ALU.add)

@@ -39,6 +39,12 @@ def tile_bertunpadselfattention_kernel(tc, table, w, b, attn_bias, offs, out):
         nc.vector.memset(warm[:], 0.0)
         nc.scalar.activation(warm[:], warm[:], ACT.Exp)
 
+        zeros = held.tile([P, P], BF16, name="zeros")
+        nc.gpsimd.memset(zeros[:], 0.0)
+        idle_ps = psum.tile([P, P], F32, name="idle_ps")
+        for _ in range(14):
+            nc.tensor.matmul(idle_ps[:], zeros[:], zeros[:], start=True, stop=True)
+
         identity = held.tile([P, P], BF16, name="identity")
         make_identity(nc, identity[:])
 
@@ -60,6 +66,9 @@ def tile_bertunpadselfattention_kernel(tc, table, w, b, attn_bias, offs, out):
         nc.tensor.transpose(vT_ps[:], v[:], identity[:])
         vT = held.tile([N, P], BF16, name="vT")
         nc.scalar.copy(vT[:], vT_ps[:])
+
+        for _ in range(8):
+            nc.tensor.matmul(idle_ps[:], qk[:], qk[:], start=True, stop=True)
 
         sc = held.tile([N, N], F32, name="sc")
         nc.vector.scalar_tensor_tensor(sc[:], dots_ps[:], SCALE, bias_sb[:], ALU.mult, ALU.add)

@@ -23,15 +23,18 @@ def tile_bertunpadselfattention_kernel(tc, table, w, b, attn_bias, offs, out):
         tc.tile_pool(name="held", bufs=1) as held,
         tc.psum_pool(name="psum", bufs=1) as psum,
     ):
+        HALF = SLOTS // 2
         offsets = held.tile([P, N // 16], U16, name="offsets")
         nc.sync.dma_start(offsets[:], offs)
-        table_sb = held.tile([P, SLOTS], BF16, name="table_sb")
-        nc.sync.dma_start(table_sb[:], table)
-        w_sb = held.tile([P, 2 * P], BF16, name="w_sb")
-        nc.scalar.dma_start(w_sb[:], w)
         b_sb = held.tile([P, 2], F32, name="b_sb")
         with nc.allow_non_contiguous_dma(reason="256 floats, one to a partition and column"):
             nc.scalar.dma_start(b_sb[:], b.rearrange("(h p) o -> p (h o)", p=P))
+        table_sb = held.tile([P, SLOTS], BF16, name="table_sb")
+        nc.sync.dma_start(table_sb[:, 0:HALF], table[:, 0:HALF])
+        nc.scalar.dma_start(table_sb[:, HALF:SLOTS], table[:, HALF:SLOTS])
+        w_sb = held.tile([P, 2 * P], BF16, name="w_sb")
+        nc.sync.dma_start(w_sb[:, 0:P], w[:, 0:P])
+        nc.scalar.dma_start(w_sb[:, P : 2 * P], w[:, P : 2 * P])
         bias_sb = held.tile([P, N], F32, name="bias_sb")
         nc.scalar.dma_start(bias_sb[:], attn_bias)
 
@@ -88,6 +91,9 @@ def tile_bertunpadselfattention_kernel(tc, table, w, b, attn_bias, offs, out):
         nc.vector.tensor_copy(pT[:], pT_ps[:])
         out_ps = psum.tile([P, N], F32, name="out_ps")
         nc.tensor.matmul(out_ps[:], vT[:], pT[:], start=True, stop=True)
+        H = P // 2
         out_sb = held.tile([P, N], F32, name="out_sb")
-        nc.vector.tensor_copy(out_sb[:], out_ps[:])
-        nc.sync.dma_start(out, out_sb[:])
+        nc.vector.tensor_copy(out_sb[0:H, :], out_ps[0:H, :])
+        nc.sync.dma_start(out[0:H, :], out_sb[0:H, :])
+        nc.scalar.copy(out_sb[H:P, :], out_ps[H:P, :])
+        nc.scalar.dma_start(out[H:P, :], out_sb[H:P, :])

@@ -23,29 +23,22 @@ def tile_bertunpadselfattention_kernel(tc, table, w, b, attn_bias, offs, out):
         tc.tile_pool(name="held", bufs=1) as held,
         tc.psum_pool(name="psum", bufs=1) as psum,
     ):
-        HALF = SLOTS // 2
         offsets = held.tile([P, N // 16], U16, name="offsets")
         nc.sync.dma_start(offsets[:], offs)
+        table_sb = held.tile([P, SLOTS], BF16, name="table_sb")
+        nc.sync.dma_start(table_sb[:], table)
+        w_sb = held.tile([P, 2 * P], BF16, name="w_sb")
+        nc.scalar.dma_start(w_sb[:], w)
         b_sb = held.tile([P, 2], F32, name="b_sb")
         with nc.allow_non_contiguous_dma(reason="256 floats, one to a partition and column"):
             nc.scalar.dma_start(b_sb[:], b.rearrange("(h p) o -> p (h o)", p=P))
-        table_sb = held.tile([P, SLOTS], BF16, name="table_sb")
-        nc.sync.dma_start(table_sb[:, 0:HALF], table[:, 0:HALF])
-        nc.scalar.dma_start(table_sb[:, HALF:SLOTS], table[:, HALF:SLOTS])
-        w_sb = held.tile([P, 2 * P], BF16, name="w_sb")
-        nc.sync.dma_start(w_sb[:, 0:P], w[:, 0:P])
-        nc.scalar.dma_start(w_sb[:, P : 2 * P], w[:, P : 2 * P])
         bias_sb = held.tile([P, N], F32, name="bias_sb")
         nc.scalar.dma_start(bias_sb[:], attn_bias)
-
-        warm = held.tile([P, 1], F32, name="warm")
-        nc.vector.memset(warm[:], 0.0)
-        nc.scalar.activation(warm[:], warm[:], ACT.Exp)
 
         zeros = held.tile([P, P], BF16, name="zeros")
         nc.gpsimd.memset(zeros[:], 0.0)
         idle_ps = psum.tile([P, P], F32, name="idle_ps")
-        for _ in range(14):
+        for _ in range(16):
             nc.tensor.matmul(idle_ps[:], zeros[:], zeros[:], start=True, stop=True)
 
         identity = held.tile([P, P], BF16, name="identity")
@@ -60,7 +53,7 @@ def tile_bertunpadselfattention_kernel(tc, table, w, b, attn_bias, offs, out):
         qk = held.tile([P, N], BF16, name="qk")
         nc.vector.tensor_scalar_add(qk[:], qk_ps[:], b_sb[:, 0:1])
         v = held.tile([P, N], BF16, name="v")
-        nc.scalar.activation(v[:], v_ps[:], ACT.Identity, bias=b_sb[:, 1:2])
+        nc.vector.tensor_scalar_add(v[:], v_ps[:], b_sb[:, 1:2])
 
         dots_ps = psum.tile([N, N], F32, name="dots_ps")
         nc.tensor.matmul(dots_ps[:], qk[:], qk[:], start=True, stop=True)
@@ -68,7 +61,7 @@ def tile_bertunpadselfattention_kernel(tc, table, w, b, attn_bias, offs, out):
         vT_ps = psum.tile([N, P], BF16, name="vT_ps")
         nc.tensor.transpose(vT_ps[:], v[:], identity[:])
         vT = held.tile([N, P], BF16, name="vT")
-        nc.scalar.copy(vT[:], vT_ps[:])
+        nc.vector.tensor_copy(vT[:], vT_ps[:])
 
         for _ in range(8):
             nc.tensor.matmul(idle_ps[:], qk[:], qk[:], start=True, stop=True)
@@ -91,9 +84,6 @@ def tile_bertunpadselfattention_kernel(tc, table, w, b, attn_bias, offs, out):
         nc.vector.tensor_copy(pT[:], pT_ps[:])
         out_ps = psum.tile([P, N], F32, name="out_ps")
         nc.tensor.matmul(out_ps[:], vT[:], pT[:], start=True, stop=True)
-        H = P // 2
         out_sb = held.tile([P, N], F32, name="out_sb")
-        nc.vector.tensor_copy(out_sb[0:H, :], out_ps[0:H, :])
-        nc.sync.dma_start(out[0:H, :], out_sb[0:H, :])
-        nc.scalar.copy(out_sb[H:P, :], out_ps[H:P, :])
-        nc.scalar.dma_start(out[H:P, :], out_sb[H:P, :])
+        nc.vector.tensor_copy(out_sb[:], out_ps[:])
+        nc.sync.dma_start(out, out_sb[:])

@@ -27,18 +27,23 @@ def tile_bertunpadselfattention_kernel(tc, table, w, b, attn_bias, offs, out):
         nc.sync.dma_start(offsets[:], offs)
         table_sb = held.tile([P, SLOTS], BF16, name="table_sb")
         nc.sync.dma_start(table_sb[:], table)
+        b_qk = held.tile([P, 1], F32, name="b_qk")
+        nc.scalar.dma_start(b_qk[:], b[0:P, :])
         w_sb = held.tile([P, 2 * P], BF16, name="w_sb")
         nc.scalar.dma_start(w_sb[:], w)
-        b_sb = held.tile([P, 2], F32, name="b_sb")
-        with nc.allow_non_contiguous_dma(reason="256 floats, one to a partition and column"):
-            nc.scalar.dma_start(b_sb[:], b.rearrange("(h p) o -> p (h o)", p=P))
+        b_v = held.tile([P, 1], F32, name="b_v")
+        nc.scalar.dma_start(b_v[:], b[P : 2 * P, :])
         bias_sb = held.tile([P, N], F32, name="bias_sb")
         nc.scalar.dma_start(bias_sb[:], attn_bias)
+
+        warm = held.tile([P, 1], F32, name="warm")
+        nc.vector.memset(warm[:], 0.0)
+        nc.scalar.activation(warm[:], warm[:], ACT.Exp)
 
         zeros = held.tile([P, P], BF16, name="zeros")
         nc.gpsimd.memset(zeros[:], 0.0)
         idle_ps = psum.tile([P, P], F32, name="idle_ps")
-        for _ in range(16):
+        for _ in range(14):
             nc.tensor.matmul(idle_ps[:], zeros[:], zeros[:], start=True, stop=True)
 
         identity = held.tile([P, P], BF16, name="identity")
@@ -51,9 +56,9 @@ def tile_bertunpadselfattention_kernel(tc, table, w, b, attn_bias, offs, out):
         nc.tensor.matmul(v_ps[:], w_sb[:, P : 2 * P], picked, start=True, stop=True)
 
         qk = held.tile([P, N], BF16, name="qk")
-        nc.vector.tensor_scalar_add(qk[:], qk_ps[:], b_sb[:, 0:1])
+        nc.vector.tensor_scalar_add(qk[:], qk_ps[:], b_qk[:])
         v = held.tile([P, N], BF16, name="v")
-        nc.vector.tensor_scalar_add(v[:], v_ps[:], b_sb[:, 1:2])
+        nc.scalar.activation(v[:], v_ps[:], ACT.Identity, bias=b_v[:])
 
         dots_ps = psum.tile([N, N], F32, name="dots_ps")
         nc.tensor.matmul(dots_ps[:], qk[:], qk[:], start=True, stop=True)
@@ -61,7 +66,7 @@ def tile_bertunpadselfattention_kernel(tc, table, w, b, attn_bias, offs, out):
         vT_ps = psum.tile([N, P], BF16, name="vT_ps")
         nc.tensor.transpose(vT_ps[:], v[:], identity[:])
         vT = held.tile([N, P], BF16, name="vT")
-        nc.vector.tensor_copy(vT[:], vT_ps[:])
+        nc.scalar.copy(vT[:], vT_ps[:])
 
         for _ in range(8):
             nc.tensor.matmul(idle_ps[:], qk[:], qk[:], start=True, stop=True)

@@ -27,14 +27,13 @@ def tile_bertunpadselfattention_kernel(tc, table, w, b, attn_bias, offs, out):
         nc.sync.dma_start(offsets[:], offs)
         table_sb = held.tile([P, SLOTS], BF16, name="table_sb")
         nc.sync.dma_start(table_sb[:], table)
-        b_qk = held.tile([P, 1], F32, name="b_qk")
-        nc.scalar.dma_start(b_qk[:], b[0:P, :])
         w_sb = held.tile([P, 2 * P], BF16, name="w_sb")
         nc.scalar.dma_start(w_sb[:], w)
-        b_v = held.tile([P, 1], F32, name="b_v")
-        nc.scalar.dma_start(b_v[:], b[P : 2 * P, :])
+        b_sb = held.tile([P, 2], F32, name="b_sb")
+        with nc.allow_non_contiguous_dma(reason="256 floats, one to a partition and column"):
+            nc.scalar.dma_start(b_sb[:], b.rearrange("(h p) o -> p (h o)", p=P))
         bias_sb = held.tile([P, N], F32, name="bias_sb")
-        nc.scalar.dma_start(bias_sb[:], attn_bias)
+        nc.sync.dma_start(bias_sb[:], attn_bias)
 
         warm = held.tile([P, 1], F32, name="warm")
         nc.vector.memset(warm[:], 0.0)
@@ -56,9 +55,9 @@ def tile_bertunpadselfattention_kernel(tc, table, w, b, attn_bias, offs, out):
         nc.tensor.matmul(v_ps[:], w_sb[:, P : 2 * P], picked, start=True, stop=True)
 
         qk = held.tile([P, N], BF16, name="qk")
-        nc.vector.tensor_scalar_add(qk[:], qk_ps[:], b_qk[:])
+        nc.vector.tensor_scalar_add(qk[:], qk_ps[:], b_sb[:, 0:1])
         v = held.tile([P, N], BF16, name="v")
-        nc.scalar.activation(v[:], v_ps[:], ACT.Identity, bias=b_v[:])
+        nc.scalar.activation(v[:], v_ps[:], ACT.Identity, bias=b_sb[:, 1:2])
 
         dots_ps = psum.tile([N, N], F32, name="dots_ps")
         nc.tensor.matmul(dots_ps[:], qk[:], qk[:], start=True, stop=True)

@@ -9,6 +9,9 @@ N = 128
 SCALE = 1.0 / math.sqrt(P)
 FLOPS = 2 * P * (2 * P) * N + 2 * P * N * N + 2 * N * N * P
 
+WARM_MATMULS = 14
+FILL_MATMULS = 8
+
 BF16 = mybir.dt.bfloat16
 F32 = mybir.dt.float32
 U16 = mybir.dt.uint16
@@ -23,16 +26,16 @@ def tile_bertunpadselfattention_kernel(tc, table, w, b, attn_bias, offs, out):
         tc.tile_pool(name="held", bufs=1) as held,
         tc.psum_pool(name="psum", bufs=1) as psum,
     ):
-        offsets = held.tile([P, N // 16], U16, name="offsets")
-        nc.sync.dma_start(offsets[:], offs)
         table_sb = held.tile([P, SLOTS], BF16, name="table_sb")
         nc.sync.dma_start(table_sb[:], table)
+        offsets = held.tile([P, N // 16], U16, name="offsets")
+        nc.sync.dma_start(offsets[:], offs)
         w_sb = held.tile([P, 2 * P], BF16, name="w_sb")
         nc.scalar.dma_start(w_sb[:], w)
         b_sb = held.tile([P, 2], F32, name="b_sb")
         with nc.allow_non_contiguous_dma(reason="256 floats, one to a partition and column"):
             nc.scalar.dma_start(b_sb[:], b.rearrange("(h p) o -> p (h o)", p=P))
-        bias_sb = held.tile([P, N], F32, name="bias_sb")
+        bias_sb = held.tile([N, N], F32, name="bias_sb")
         nc.sync.dma_start(bias_sb[:], attn_bias)
 
         warm = held.tile([P, 1], F32, name="warm")
@@ -42,7 +45,7 @@ def tile_bertunpadselfattention_kernel(tc, table, w, b, attn_bias, offs, out):
         zeros = held.tile([P, P], BF16, name="zeros")
         nc.gpsimd.memset(zeros[:], 0.0)
         idle_ps = psum.tile([P, P], F32, name="idle_ps")
-        for _ in range(14):
+        for _ in range(WARM_MATMULS):
             nc.tensor.matmul(idle_ps[:], zeros[:], zeros[:], start=True, stop=True)
 
         identity = held.tile([P, P], BF16, name="identity")
@@ -67,7 +70,7 @@ def tile_bertunpadselfattention_kernel(tc, table, w, b, attn_bias, offs, out):
         vT = held.tile([N, P], BF16, name="vT")
         nc.scalar.copy(vT[:], vT_ps[:])
 
-        for _ in range(8):
+        for _ in range(FILL_MATMULS):
             nc.tensor.matmul(idle_ps[:], qk[:], qk[:], start=True, stop=True)
 
         sc = held.tile([N, N], F32, name="sc")

@@ -7,10 +7,11 @@ P = 128
 SLOTS = 512
 N = 128
 SCALE = 1.0 / math.sqrt(P)
+QK_SCALE = math.sqrt(SCALE)
 FLOPS = 2 * P * (2 * P) * N + 2 * P * N * N + 2 * N * N * P
 
 WARM_MATMULS = 14
-FILL_MATMULS = 8
+FILL_MATMULS = 2
 
 BF16 = mybir.dt.bfloat16
 F32 = mybir.dt.float32
@@ -50,6 +51,8 @@ def tile_bertunpadselfattention_kernel(tc, table, w, b, attn_bias, offs, out):
 
         identity = held.tile([P, P], BF16, name="identity")
         make_identity(nc, identity[:])
+        identity_f32 = held.tile([P, P], F32, name="identity_f32")
+        make_identity(nc, identity_f32[:])
 
         picked = table_sb[:].indirect(offsets[:])
         qk_ps = psum.tile([P, N], F32, name="qk_ps")
@@ -58,39 +61,40 @@ def tile_bertunpadselfattention_kernel(tc, table, w, b, attn_bias, offs, out):
         nc.tensor.matmul(v_ps[:], w_sb[:, P : 2 * P], picked, start=True, stop=True)
 
         qk = held.tile([P, N], BF16, name="qk")
-        nc.vector.tensor_scalar_add(qk[:], qk_ps[:], b_sb[:, 0:1])
+        nc.vector.tensor_scalar(qk[:], qk_ps[:], b_sb[:, 0:1], QK_SCALE, ALU.add, ALU.mult)
         v = held.tile([P, N], BF16, name="v")
         nc.scalar.activation(v[:], v_ps[:], ACT.Identity, bias=b_sb[:, 1:2])
 
-        dots_ps = psum.tile([N, N], F32, name="dots_ps")
-        nc.tensor.matmul(dots_ps[:], qk[:], qk[:], start=True, stop=True)
+        sc_ps = psum.tile([N, N], F32, name="sc_ps")
+        nc.tensor.matmul(sc_ps[:], identity_f32[:], bias_sb[:], start=True, stop=False)
+        nc.tensor.matmul(sc_ps[:], qk[:], qk[:], start=False, stop=True)
 
         vT_ps = psum.tile([N, P], BF16, name="vT_ps")
         nc.tensor.transpose(vT_ps[:], v[:], identity[:])
-        vT = held.tile([N, P], BF16, name="vT")
-        nc.scalar.copy(vT[:], vT_ps[:])
 
         for _ in range(FILL_MATMULS):
             nc.tensor.matmul(idle_ps[:], qk[:], qk[:], start=True, stop=True)
 
-        sc = held.tile([N, N], F32, name="sc")
-        nc.vector.scalar_tensor_tensor(sc[:], dots_ps[:], SCALE, bias_sb[:], ALU.mult, ALU.add)
         neg_max = held.tile([N, 1], F32, name="neg_max")
-        nc.vector.reduce_max(neg_max[:], sc[:], axis=X, negate=True)
-        e = held.tile([N, N], F32, name="e")
+        nc.vector.reduce_max(neg_max[:], sc_ps[:], axis=X, negate=True)
+        vT = held.tile([N, P], BF16, name="vT")
+        nc.vector.tensor_copy(vT[:], vT_ps[:])
+        e = held.tile([N, N], BF16, name="e")
         e_sum = held.tile([N, 1], F32, name="e_sum")
-        nc.scalar.activation(e[:], sc[:], ACT.Exp, bias=neg_max[:], scale=1.0, accum_out=e_sum[:])
+        nc.scalar.activation(e[:], sc_ps[:], ACT.Exp, bias=neg_max[:], scale=1.0, accum_out=e_sum[:])
+
+        eT_ps = psum.tile([N, N], BF16, name="eT_ps")
+        nc.tensor.transpose(eT_ps[:], e[:], identity[:])
         inv_sum = held.tile([N, 1], F32, name="inv_sum")
         nc.vector.reciprocal(inv_sum[:], e_sum[:])
-        p = held.tile([N, N], BF16, name="p")
-        nc.vector.tensor_scalar_mul(p[:], e[:], inv_sum[:])
-
-        pT_ps = psum.tile([N, N], BF16, name="pT_ps")
-        nc.tensor.transpose(pT_ps[:], p[:], identity[:])
-        pT = held.tile([N, N], BF16, name="pT")
-        nc.vector.tensor_copy(pT[:], pT_ps[:])
+        inv_ps = psum.tile([P, N], F32, name="inv_ps")
+        nc.tensor.transpose(inv_ps[:], inv_sum[:, 0:1].to_broadcast([N, P]), identity_f32[:])
+        eT = held.tile([N, N], BF16, name="eT")
+        nc.vector.tensor_copy(eT[:], eT_ps[:])
+        inv_rows = held.tile([P, N], F32, name="inv_rows")
+        nc.scalar.copy(inv_rows[:], inv_ps[:])
         out_ps = psum.tile([P, N], F32, name="out_ps")
-        nc.tensor.matmul(out_ps[:], vT[:], pT[:], start=True, stop=True)
+        nc.tensor.matmul(out_ps[:], vT[:], eT[:], start=True, stop=True)
         out_sb = held.tile([P, N], F32, name="out_sb")
-        nc.vector.tensor_copy(out_sb[:], out_ps[:])
+        nc.vector.tensor_tensor(out_sb[:], out_ps[:], inv_rows[:], ALU.mult)
         nc.sync.dma_start(out, out_sb[:])

@@ -65,9 +65,8 @@ def tile_bertunpadselfattention_kernel(tc, table, w, b, attn_bias, offs, out):
         v = held.tile([P, N], BF16, name="v")
         nc.scalar.activation(v[:], v_ps[:], ACT.Identity, bias=b_sb[:, 1:2])
 
-        sc_ps = psum.tile([N, N], F32, name="sc_ps")
-        nc.tensor.matmul(sc_ps[:], identity_f32[:], bias_sb[:], start=True, stop=False)
-        nc.tensor.matmul(sc_ps[:], qk[:], qk[:], start=False, stop=True)
+        dots_ps = psum.tile([N, N], F32, name="dots_ps")
+        nc.tensor.matmul(dots_ps[:], qk[:], qk[:], start=True, stop=True)
 
         vT_ps = psum.tile([N, P], BF16, name="vT_ps")
         nc.tensor.transpose(vT_ps[:], v[:], identity[:])
@@ -75,13 +74,15 @@ def tile_bertunpadselfattention_kernel(tc, table, w, b, attn_bias, offs, out):
         for _ in range(FILL_MATMULS):
             nc.tensor.matmul(idle_ps[:], qk[:], qk[:], start=True, stop=True)
 
+        sc = held.tile([N, N], F32, name="sc")
+        nc.vector.tensor_tensor(sc[:], dots_ps[:], bias_sb[:], ALU.add)
         neg_max = held.tile([N, 1], F32, name="neg_max")
-        nc.vector.reduce_max(neg_max[:], sc_ps[:], axis=X, negate=True)
+        nc.vector.reduce_max(neg_max[:], sc[:], axis=X, negate=True)
         vT = held.tile([N, P], BF16, name="vT")
         nc.vector.tensor_copy(vT[:], vT_ps[:])
         e = held.tile([N, N], BF16, name="e")
         e_sum = held.tile([N, 1], F32, name="e_sum")
-        nc.scalar.activation(e[:], sc_ps[:], ACT.Exp, bias=neg_max[:], scale=1.0, accum_out=e_sum[:])
+        nc.scalar.activation(e[:], sc[:], ACT.Exp, bias=neg_max[:], scale=1.0, accum_out=e_sum[:])
 
         eT_ps = psum.tile([N, N], BF16, name="eT_ps")
         nc.tensor.transpose(eT_ps[:], e[:], identity[:])

@@ -8,10 +8,10 @@ SLOTS = 512
 N = 128
 SCALE = 1.0 / math.sqrt(P)
 QK_SCALE = math.sqrt(SCALE)
+FINITE = 3.0e38
 FLOPS = 2 * P * (2 * P) * N + 2 * P * N * N + 2 * N * N * P
 
 WARM_MATMULS = 14
-FILL_MATMULS = 2
 
 BF16 = mybir.dt.bfloat16
 F32 = mybir.dt.float32
@@ -31,13 +31,15 @@ def tile_bertunpadselfattention_kernel(tc, table, w, b, attn_bias, offs, out):
         nc.sync.dma_start(table_sb[:], table)
         offsets = held.tile([P, N // 16], U16, name="offsets")
         nc.sync.dma_start(offsets[:], offs)
-        w_sb = held.tile([P, 2 * P], BF16, name="w_sb")
-        nc.scalar.dma_start(w_sb[:], w)
+        bias_sb = held.tile([N, N], F32, name="bias_sb")
+        nc.scalar.dma_start(bias_sb[:], attn_bias)
+        w_qk = held.tile([P, P], BF16, name="w_qk")
+        nc.scalar.dma_start(w_qk[:], w[:, 0:P])
+        w_v = held.tile([P, P], BF16, name="w_v")
+        nc.scalar.dma_start(w_v[:], w[:, P : 2 * P])
         b_sb = held.tile([P, 2], F32, name="b_sb")
         with nc.allow_non_contiguous_dma(reason="256 floats, one to a partition and column"):
-            nc.scalar.dma_start(b_sb[:], b.rearrange("(h p) o -> p (h o)", p=P))
-        bias_sb = held.tile([N, N], F32, name="bias_sb")
-        nc.sync.dma_start(bias_sb[:], attn_bias)
+            nc.sync.dma_start(b_sb[:], b.rearrange("(h p) o -> p (h o)", p=P))
 
         warm = held.tile([P, 1], F32, name="warm")
         nc.vector.memset(warm[:], 0.0)
@@ -54,35 +56,42 @@ def tile_bertunpadselfattention_kernel(tc, table, w, b, attn_bias, offs, out):
         identity_f32 = held.tile([P, P], F32, name="identity_f32")
         make_identity(nc, identity_f32[:])
 
+        bias_fin = held.tile([N, N], F32, name="bias_fin")
+        nc.vector.tensor_scalar(bias_fin[:], bias_sb[:], -FINITE, FINITE, ALU.max, ALU.min)
+        bias_hi = bias_fin[:].bitcast(BF16)[:, 1 : 2 * N : 2]
+        rest = held.tile([N, N], F32, name="rest")
+        nc.vector.tensor_tensor(rest[:], bias_fin[:], bias_hi, ALU.subtract)
+        rest_hi = rest[:].bitcast(BF16)[:, 1 : 2 * N : 2]
+        rest_lo = held.tile([N, N], BF16, name="rest_lo")
+        nc.vector.tensor_tensor(rest_lo[:], rest[:], rest_hi, ALU.subtract)
+
         picked = table_sb[:].indirect(offsets[:])
         qk_ps = psum.tile([P, N], F32, name="qk_ps")
-        nc.tensor.matmul(qk_ps[:], w_sb[:, 0:P], picked, start=True, stop=True)
+        nc.tensor.matmul(qk_ps[:], w_qk[:], picked, start=True, stop=True)
         v_ps = psum.tile([P, N], F32, name="v_ps")
-        nc.tensor.matmul(v_ps[:], w_sb[:, P : 2 * P], picked, start=True, stop=True)
+        nc.tensor.matmul(v_ps[:], w_v[:], picked, start=True, stop=True)
 
         qk = held.tile([P, N], BF16, name="qk")
         nc.vector.tensor_scalar(qk[:], qk_ps[:], b_sb[:, 0:1], QK_SCALE, ALU.add, ALU.mult)
         v = held.tile([P, N], BF16, name="v")
         nc.scalar.activation(v[:], v_ps[:], ACT.Identity, bias=b_sb[:, 1:2])
 
-        dots_ps = psum.tile([N, N], F32, name="dots_ps")
-        nc.tensor.matmul(dots_ps[:], qk[:], qk[:], start=True, stop=True)
+        sc_ps = psum.tile([N, N], F32, name="sc_ps")
+        nc.tensor.matmul(sc_ps[:], identity[:], bias_hi, start=True, stop=False)
+        nc.tensor.matmul(sc_ps[:], identity[:], rest_hi, start=False, stop=False)
+        nc.tensor.matmul(sc_ps[:], identity[:], rest_lo[:], start=False, stop=False)
+        nc.tensor.matmul(sc_ps[:], qk[:], qk[:], start=False, stop=True)
 
         vT_ps = psum.tile([N, P], BF16, name="vT_ps")
         nc.tensor.transpose(vT_ps[:], v[:], identity[:])
 
-        for _ in range(FILL_MATMULS):
-            nc.tensor.matmul(idle_ps[:], qk[:], qk[:], start=True, stop=True)
-
-        sc = held.tile([N, N], F32, name="sc")
-        nc.vector.tensor_tensor(sc[:], dots_ps[:], bias_sb[:], ALU.add)
         neg_max = held.tile([N, 1], F32, name="neg_max")
-        nc.vector.reduce_max(neg_max[:], sc[:], axis=X, negate=True)
+        nc.vector.reduce_max(neg_max[:], sc_ps[:], axis=X, negate=True)
         vT = held.tile([N, P], BF16, name="vT")
         nc.vector.tensor_copy(vT[:], vT_ps[:])
         e = held.tile([N, N], BF16, name="e")
         e_sum = held.tile([N, 1], F32, name="e_sum")
-        nc.scalar.activation(e[:], sc[:], ACT.Exp, bias=neg_max[:], scale=1.0, accum_out=e_sum[:])
+        nc.scalar.activation(e[:], sc_ps[:], ACT.Exp, bias=neg_max[:], scale=1.0, accum_out=e_sum[:])
 
         eT_ps = psum.tile([N, N], BF16, name="eT_ps")
         nc.tensor.transpose(eT_ps[:], e[:], identity[:])

@@ -27,16 +27,14 @@ def tile_bertunpadselfattention_kernel(tc, table, w, b, attn_bias, offs, out):
         tc.tile_pool(name="held", bufs=1) as held,
         tc.psum_pool(name="psum", bufs=1) as psum,
     ):
+        bias_sb = held.tile([N, N], F32, name="bias_sb")
+        nc.sync.dma_start(bias_sb[:], attn_bias)
         table_sb = held.tile([P, SLOTS], BF16, name="table_sb")
-        nc.sync.dma_start(table_sb[:], table)
+        nc.scalar.dma_start(table_sb[:], table)
         offsets = held.tile([P, N // 16], U16, name="offsets")
         nc.sync.dma_start(offsets[:], offs)
-        bias_sb = held.tile([N, N], F32, name="bias_sb")
-        nc.scalar.dma_start(bias_sb[:], attn_bias)
-        w_qk = held.tile([P, P], BF16, name="w_qk")
-        nc.scalar.dma_start(w_qk[:], w[:, 0:P])
-        w_v = held.tile([P, P], BF16, name="w_v")
-        nc.scalar.dma_start(w_v[:], w[:, P : 2 * P])
+        w_sb = held.tile([P, 2 * P], BF16, name="w_sb")
+        nc.scalar.dma_start(w_sb[:], w)
         b_sb = held.tile([P, 2], F32, name="b_sb")
         with nc.allow_non_contiguous_dma(reason="256 floats, one to a partition and column"):
             nc.sync.dma_start(b_sb[:], b.rearrange("(h p) o -> p (h o)", p=P))
@@ -67,9 +65,9 @@ def tile_bertunpadselfattention_kernel(tc, table, w, b, attn_bias, offs, out):
 
         picked = table_sb[:].indirect(offsets[:])
         qk_ps = psum.tile([P, N], F32, name="qk_ps")
-        nc.tensor.matmul(qk_ps[:], w_qk[:], picked, start=True, stop=True)
+        nc.tensor.matmul(qk_ps[:], w_sb[:, 0:P], picked, start=True, stop=True)
         v_ps = psum.tile([P, N], F32, name="v_ps")
-        nc.tensor.matmul(v_ps[:], w_v[:], picked, start=True, stop=True)
+        nc.tensor.matmul(v_ps[:], w_sb[:, P : 2 * P], picked, start=True, stop=True)
 
         qk = held.tile([P, N], BF16, name="qk")
         nc.vector.tensor_scalar(qk[:], qk_ps[:], b_sb[:, 0:1], QK_SCALE, ALU.add, ALU.mult)

@@ -27,14 +27,14 @@ def tile_bertunpadselfattention_kernel(tc, table, w, b, attn_bias, offs, out):
         tc.tile_pool(name="held", bufs=1) as held,
         tc.psum_pool(name="psum", bufs=1) as psum,
     ):
-        bias_sb = held.tile([N, N], F32, name="bias_sb")
-        nc.sync.dma_start(bias_sb[:], attn_bias)
         table_sb = held.tile([P, SLOTS], BF16, name="table_sb")
-        nc.scalar.dma_start(table_sb[:], table)
-        offsets = held.tile([P, N // 16], U16, name="offsets")
-        nc.sync.dma_start(offsets[:], offs)
+        nc.sync.dma_start(table_sb[:], table)
         w_sb = held.tile([P, 2 * P], BF16, name="w_sb")
         nc.scalar.dma_start(w_sb[:], w)
+        offsets = held.tile([P, N // 16], U16, name="offsets")
+        nc.sync.dma_start(offsets[:], offs)
+        bias_sb = held.tile([N, N], F32, name="bias_sb")
+        nc.scalar.dma_start(bias_sb[:], attn_bias)
         b_sb = held.tile([P, 2], F32, name="b_sb")
         with nc.allow_non_contiguous_dma(reason="256 floats, one to a partition and column"):
             nc.sync.dma_start(b_sb[:], b.rearrange("(h p) o -> p (h o)", p=P))
@@ -49,19 +49,13 @@ def tile_bertunpadselfattention_kernel(tc, table, w, b, attn_bias, offs, out):
         for _ in range(WARM_MATMULS):
             nc.tensor.matmul(idle_ps[:], zeros[:], zeros[:], start=True, stop=True)
 
-        identity = held.tile([P, P], BF16, name="identity")
-        make_identity(nc, identity[:])
         identity_f32 = held.tile([P, P], F32, name="identity_f32")
         make_identity(nc, identity_f32[:])
+        identity = held.tile([P, P], BF16, name="identity")
+        make_identity(nc, identity[:])
 
         bias_fin = held.tile([N, N], F32, name="bias_fin")
         nc.vector.tensor_scalar(bias_fin[:], bias_sb[:], -FINITE, FINITE, ALU.max, ALU.min)
-        bias_hi = bias_fin[:].bitcast(BF16)[:, 1 : 2 * N : 2]
-        rest = held.tile([N, N], F32, name="rest")
-        nc.vector.tensor_tensor(rest[:], bias_fin[:], bias_hi, ALU.subtract)
-        rest_hi = rest[:].bitcast(BF16)[:, 1 : 2 * N : 2]
-        rest_lo = held.tile([N, N], BF16, name="rest_lo")
-        nc.vector.tensor_tensor(rest_lo[:], rest[:], rest_hi, ALU.subtract)
 
         picked = table_sb[:].indirect(offsets[:])
         qk_ps = psum.tile([P, N], F32, name="qk_ps")
@@ -75,9 +69,7 @@ def tile_bertunpadselfattention_kernel(tc, table, w, b, attn_bias, offs, out):
         nc.scalar.activation(v[:], v_ps[:], ACT.Identity, bias=b_sb[:, 1:2])
 
         sc_ps = psum.tile([N, N], F32, name="sc_ps")
-        nc.tensor.matmul(sc_ps[:], identity[:], bias_hi, start=True, stop=False)
-        nc.tensor.matmul(sc_ps[:], identity[:], rest_hi, start=False, stop=False)
-        nc.tensor.matmul(sc_ps[:], identity[:], rest_lo[:], start=False, stop=False)
+        nc.tensor.matmul(sc_ps[:], identity_f32[:], bias_fin[:], start=True, stop=False)
         nc.tensor.matmul(sc_ps[:], qk[:], qk[:], start=False, stop=True)
 
         vT_ps = psum.tile([N, P], BF16, name="vT_ps")

@@ -11,7 +11,7 @@ QK_SCALE = math.sqrt(SCALE)
 FINITE = 3.0e38
 FLOPS = 2 * P * (2 * P) * N + 2 * P * N * N + 2 * N * N * P
 
-WARM_MATMULS = 14
+WARM_MATMULS = 16
 
 BF16 = mybir.dt.bfloat16
 F32 = mybir.dt.float32
@@ -39,15 +39,17 @@ def tile_bertunpadselfattention_kernel(tc, table, w, b, attn_bias, offs, out):
         with nc.allow_non_contiguous_dma(reason="256 floats, one to a partition and column"):
             nc.sync.dma_start(b_sb[:], b.rearrange("(h p) o -> p (h o)", p=P))
 
+        zero = held.tile([P, 1], BF16, name="zero")
+        nc.gpsimd.memset(zero[:], 0.0)
+        zeros = zero[:, 0:1].to_broadcast([P, P])
+        idle_ps = psum.tile([P, P], F32, name="idle_ps")
+        for _ in range(WARM_MATMULS):
+            nc.tensor.matmul(idle_ps[:], zeros, zeros, start=True, stop=True)
+
         warm = held.tile([P, 1], F32, name="warm")
         nc.vector.memset(warm[:], 0.0)
         nc.scalar.activation(warm[:], warm[:], ACT.Exp)
 
-        zeros = held.tile([P, P], BF16, name="zeros")
-        nc.gpsimd.memset(zeros[:], 0.0)
-        idle_ps = psum.tile([P, P], F32, name="idle_ps")
-        for _ in range(WARM_MATMULS):
-            nc.tensor.matmul(idle_ps[:], zeros[:], zeros[:], start=True, stop=True)
 
         identity_f32 = held.tile([P, P], F32, name="identity_f32")
         make_identity(nc, identity_f32[:])

@@ -12,6 +12,7 @@ FINITE = 3.0e38
 FLOPS = 2 * P * (2 * P) * N + 2 * P * N * N + 2 * N * N * P
 
 WARM_MATMULS = 16
+FILL_MATMULS = 4
 
 BF16 = mybir.dt.bfloat16
 F32 = mybir.dt.float32
@@ -50,7 +51,6 @@ def tile_bertunpadselfattention_kernel(tc, table, w, b, attn_bias, offs, out):
         nc.vector.memset(warm[:], 0.0)
         nc.scalar.activation(warm[:], warm[:], ACT.Exp)
 
-
         identity_f32 = held.tile([P, P], F32, name="identity_f32")
         make_identity(nc, identity_f32[:])
         identity = held.tile([P, P], BF16, name="identity")
@@ -76,6 +76,8 @@ def tile_bertunpadselfattention_kernel(tc, table, w, b, attn_bias, offs, out):
 
         vT_ps = psum.tile([N, P], BF16, name="vT_ps")
         nc.tensor.transpose(vT_ps[:], v[:], identity[:])
+        for _ in range(FILL_MATMULS):
+            nc.tensor.matmul(idle_ps[:], identity[:], v[:], start=True, stop=True)
 
         neg_max = held.tile([N, 1], F32, name="neg_max")
         nc.vector.reduce_max(neg_max[:], sc_ps[:], axis=X, negate=True)

@@ -11,7 +11,7 @@ QK_SCALE = math.sqrt(SCALE)
 FINITE = 3.0e38
 FLOPS = 2 * P * (2 * P) * N + 2 * P * N * N + 2 * N * N * P
 
-WARM_MATMULS = 16
+WARM_MATMULS = 12
 FILL_MATMULS = 4
 
 BF16 = mybir.dt.bfloat16

@@ -94,7 +94,7 @@ def tile_bertunpadselfattention_kernel(tc, table, w, b, attn_bias, offs, out):
         inv_ps = psum.tile([P, N], F32, name="inv_ps")
         nc.tensor.transpose(inv_ps[:], inv_sum[:, 0:1].to_broadcast([N, P]), identity_f32[:])
         eT = held.tile([N, N], BF16, name="eT")
-        nc.vector.tensor_copy(eT[:], eT_ps[:])
+        nc.scalar.copy(eT[:], eT_ps[:])
         inv_rows = held.tile([P, N], F32, name="inv_rows")
         nc.scalar.copy(inv_rows[:], inv_ps[:])
         out_ps = psum.tile([P, N], F32, name="out_ps")

import math

import concourse.mybir as mybir
from concourse.masks import make_identity

P = 128
SLOTS = 512
N = 128
SCALE = 1.0 / math.sqrt(P)
QK_SCALE = math.sqrt(SCALE)
FINITE = 3.0e38
FLOPS = 2 * P * (2 * P) * N + 2 * P * N * N + 2 * N * N * P

WARM_MATMULS = 12
FILL_MATMULS = 4

BF16 = mybir.dt.bfloat16
F32 = mybir.dt.float32
U16 = mybir.dt.uint16
ALU = mybir.AluOpType
ACT = mybir.ActivationFunctionType
X = mybir.AxisListType.X


def tile_bertunpadselfattention_kernel(tc, table, w, b, attn_bias, offs, out):
    nc = tc.nc
    with (
        tc.tile_pool(name="held", bufs=1) as held,
        tc.psum_pool(name="psum", bufs=1) as psum,
    ):
        table_sb = held.tile([P, SLOTS], BF16, name="table_sb")
        nc.sync.dma_start(table_sb[:], table)
        w_sb = held.tile([P, 2 * P], BF16, name="w_sb")
        nc.scalar.dma_start(w_sb[:], w)
        offsets = held.tile([P, N // 16], U16, name="offsets")
        nc.sync.dma_start(offsets[:], offs)
        bias_sb = held.tile([N, N], F32, name="bias_sb")
        nc.scalar.dma_start(bias_sb[:], attn_bias)
        b_sb = held.tile([P, 2], F32, name="b_sb")
        with nc.allow_non_contiguous_dma(reason="256 floats, one to a partition and column"):
            nc.sync.dma_start(b_sb[:], b.rearrange("(h p) o -> p (h o)", p=P))

        zero = held.tile([P, 1], BF16, name="zero")
        nc.gpsimd.memset(zero[:], 0.0)
        zeros = zero[:, 0:1].to_broadcast([P, P])
        idle_ps = psum.tile([P, P], F32, name="idle_ps")
        for _ in range(WARM_MATMULS):
            nc.tensor.matmul(idle_ps[:], zeros, zeros, start=True, stop=True)

        warm = held.tile([P, 1], F32, name="warm")
        nc.vector.memset(warm[:], 0.0)
        nc.scalar.activation(warm[:], warm[:], ACT.Exp)

        identity_f32 = held.tile([P, P], F32, name="identity_f32")
        make_identity(nc, identity_f32[:])
        identity = held.tile([P, P], BF16, name="identity")
        make_identity(nc, identity[:])

        bias_fin = held.tile([N, N], F32, name="bias_fin")
        nc.vector.tensor_scalar(bias_fin[:], bias_sb[:], -FINITE, FINITE, ALU.max, ALU.min)

        picked = table_sb[:].indirect(offsets[:])
        qk_ps = psum.tile([P, N], F32, name="qk_ps")
        nc.tensor.matmul(qk_ps[:], w_sb[:, 0:P], picked, start=True, stop=True)
        v_ps = psum.tile([P, N], F32, name="v_ps")
        nc.tensor.matmul(v_ps[:], w_sb[:, P : 2 * P], picked, start=True, stop=True)

        qk = held.tile([P, N], BF16, name="qk")
        nc.vector.tensor_scalar(qk[:], qk_ps[:], b_sb[:, 0:1], QK_SCALE, ALU.add, ALU.mult)
        v = held.tile([P, N], BF16, name="v")
        nc.scalar.activation(v[:], v_ps[:], ACT.Identity, bias=b_sb[:, 1:2])

        sc_ps = psum.tile([N, N], F32, name="sc_ps")
        nc.tensor.matmul(sc_ps[:], identity_f32[:], bias_fin[:], start=True, stop=False)
        nc.tensor.matmul(sc_ps[:], qk[:], qk[:], start=False, stop=True)

        vT_ps = psum.tile([N, P], BF16, name="vT_ps")
        nc.tensor.transpose(vT_ps[:], v[:], identity[:])
        for _ in range(FILL_MATMULS):
            nc.tensor.matmul(idle_ps[:], identity[:], v[:], start=True, stop=True)

        neg_max = held.tile([N, 1], F32, name="neg_max")
        nc.vector.reduce_max(neg_max[:], sc_ps[:], axis=X, negate=True)
        vT = held.tile([N, P], BF16, name="vT")
        nc.vector.tensor_copy(vT[:], vT_ps[:])
        e = held.tile([N, N], BF16, name="e")
        e_sum = held.tile([N, 1], F32, name="e_sum")
        nc.scalar.activation(e[:], sc_ps[:], ACT.Exp, bias=neg_max[:], scale=1.0, accum_out=e_sum[:])

        eT_ps = psum.tile([N, N], BF16, name="eT_ps")
        nc.tensor.transpose(eT_ps[:], e[:], identity[:])
        inv_sum = held.tile([N, 1], F32, name="inv_sum")
        nc.vector.reciprocal(inv_sum[:], e_sum[:])
        inv_ps = psum.tile([P, N], F32, name="inv_ps")
        nc.tensor.transpose(inv_ps[:], inv_sum[:, 0:1].to_broadcast([N, P]), identity_f32[:])
        eT = held.tile([N, N], BF16, name="eT")
        nc.scalar.copy(eT[:], eT_ps[:])
        inv_rows = held.tile([P, N], F32, name="inv_rows")
        nc.scalar.copy(inv_rows[:], inv_ps[:])
        out_ps = psum.tile([P, N], F32, name="out_ps")
        nc.tensor.matmul(out_ps[:], vT[:], eT[:], start=True, stop=True)
        out_sb = held.tile([P, N], F32, name="out_sb")
        nc.vector.tensor_tensor(out_sb[:], out_ps[:], inv_rows[:], ALU.mult)
        nc.sync.dma_start(out, out_sb[:])
